import numpy as np
import ml_dtypes


def mxq(x, axis, fmt="e4m3"):
    dtype, down = {"e4m3": (ml_dtypes.float8_e4m3fn, 7), "e5m2": (ml_dtypes.float8_e5m2, 14)}[fmt]
    v = np.moveaxis(np.asarray(x, np.float32).astype(ml_dtypes.bfloat16).astype(np.float64), axis, -1)
    blocks = v.reshape(v.shape[:-1] + (-1, 32))
    amax = np.abs(blocks).max(-1, keepdims=True)
    byte = np.maximum(np.where(amax > 0, np.frexp(amax)[1] - 1 + 127, 0) - down, 1)
    scale = np.exp2(byte - 127.0)
    codes = (blocks / scale).astype(np.float32).astype(dtype).astype(np.float64)
    return np.moveaxis((codes * scale).reshape(v.shape), -1, axis)


WIDE = False


def mx_kscale(k):
    if not WIDE:
        return np.ones(k)
    levels = np.array([10, -10, 5, -5, 0])
    if k % 512:
        return np.exp2(np.random.permutation(np.resize(levels, k // 32))).repeat(32)
    a = np.empty((k // 512, 16))
    for p in range(k // 512):
        a[p, :8] = np.random.permutation(np.resize(levels, 8))
        for g in range(8):
            far = levels[np.abs(levels - a[p, g]) >= 10]
            a[p, g + 8] = far[np.random.randint(len(far))]
    return np.exp2(a.ravel()).repeat(32)


BF16 = ml_dtypes.bfloat16


def bf(x):
    return np.asarray(x, np.float32).astype(BF16)


def f64(x):
    return np.asarray(x).astype(np.float64)


B, L, D, H, KV, HD, QB = 4, 2048, 1024, 2, 2, 64, 512
EPS_RMS = 1e-6
EPS_NORM = 1e-12


def rmsnorm(x, w):
    var = np.mean(np.square(x), axis=-1, keepdims=True)
    return x * (1.0 / np.sqrt(var + EPS_RMS)) * w


def l2norm(x):
    n = np.sqrt(np.sum(np.square(x), axis=-1, keepdims=True))
    return x / np.maximum(n, EPS_NORM)


def heads(y, n):
    return y.reshape(B, L, n, HD).transpose(0, 2, 1, 3)


def setup_inputs():
    s = mx_kscale(D)
    c = 1.0 / np.sqrt(D)
    return {"x": bf(np.random.standard_normal((B, L, D)) * np.exp(0.5 * np.random.standard_normal((B, L, 1)))),
            "norm_w": bf((1.0 + 0.1 * np.random.standard_normal(D)) * s),
            "Wq": bf(np.random.standard_normal((D, H * HD)) * c / s[:, None]),
            "Wk": bf(np.random.standard_normal((D, KV * HD)) * c / s[:, None]),
            "Wv": bf(np.random.standard_normal((D, KV * HD)) * c / s[:, None])}


def reference(x, norm_w, Wq, Wk, Wv):
    h = mxq(rmsnorm(f64(x), f64(norm_w)), 2, "e4m3")
    q = heads(h @ mxq(f64(Wq), 0, "e4m3"), H)
    k = heads(h @ mxq(f64(Wk), 0, "e4m3"), KV)
    v = heads(h @ mxq(f64(Wv), 0, "e4m3"), KV)
    return l2norm(q), l2norm(k), v

@@ -1,0 +1,276 @@
+from contextlib import ExitStack
+
+import concourse.mybir as mybir
+from concourse.masks import make_identity
+
+F32 = mybir.dt.float32
+BF16 = mybir.dt.bfloat16
+U32 = mybir.dt.uint32
+U8 = mybir.dt.uint8
+FP8X4 = mybir.dt.float8_e4m3fn_x4
+ACT = mybir.ActivationFunctionType
+ALU = mybir.AluOpType
+
+P = 128
+B, L, D = 4, 2048, 1024
+HD = 64
+J = L // P
+GROUP = 4
+N_TILES = B * J
+N_GROUPS = N_TILES // GROUP
+FLOPS = 2 * B * L * D * 384
+
+LOAD_LEAD = 11
+SUMSQ_LEAD = 7
+Y_LEAD = 3
+G_K = 88
+
+
+def tile_sharedglobalattention_pa_t_kernel(tc, x, norm_w, Wq, Wk, Wv, out_0, out_1, out_2):
+    nc = tc.nc
+    with ExitStack() as ctx:
+        const = ctx.enter_context(tc.tile_pool(name="const", bufs=1))
+        xpool = ctx.enter_context(tc.tile_pool(name="xin", bufs=4))
+        junkp = ctx.enter_context(tc.tile_pool(name="junk", bufs=2))
+        small = ctx.enter_context(tc.tile_pool(name="small", bufs=8))
+        ypool = ctx.enter_context(tc.tile_pool(name="ytok", bufs=5))
+        gpool = ctx.enter_context(tc.tile_pool(name="grouped", bufs=3))
+        opool = ctx.enter_context(tc.tile_pool(name="outs", bufs=3))
+        ps_t = ctx.enter_context(tc.psum_pool(name="ps_t", bufs=4))
+        ps_o = ctx.enter_context(tc.psum_pool(name="ps_o", bufs=4))
+        ctx.enter_context(tc.manual_schedule())
+
+        xv = [x[b].rearrange("(p j) d -> p j d", j=J) for b in range(B)]
+        outs = (out_0, out_1, out_2)
+        ov = [[o[b].rearrange("n (p j) d -> p n j d", j=J) for b in range(B)] for o in outs]
+
+        xg, ss, rstd, ys, yts, grps, cds, pos, ssqs, rns, otile = {}, {}, {}, {}, {}, {}, {}, {}, {}, {}, {}
+
+        w4 = const.tile([P, 2, 4], BF16, name="w4")
+
+        def load(g):
+            b, j0 = divmod(g * GROUP, J)
+            t = xpool.tile([P, GROUP, D], BF16, name="xg")
+            xg[g] = t
+            if g == 0:
+                for jj in range(GROUP):
+                    nc.sync.dma_start(out=t[:, jj : jj + 1, :], in_=xv[b][:, j0 + jj : j0 + jj + 1, :])
+                    if jj == 0:
+                        nc.sync.dma_start(out=w4[:], in_=norm_w.rearrange("(c p t) -> p c t", p=P, t=4))
+            else:
+                nc.sync.dma_start(out=t[:], in_=xv[b][:, j0 : j0 + GROUP, :])
+
+        load(0)
+
+        wraw = const.tile([P, 3, 2, 512], BF16, name="wraw")
+        for m, w in enumerate((Wq, Wk, Wv)):
+            nc.scalar.dma_start(out=wraw[:, m], in_=w.rearrange("(c p t) n -> p c (t n)", p=P, t=4))
+        eps_t = const.tile([P, 1], F32, name="eps_t")
+        nc.vector.memset(eps_t[:], 1e-6)
+        tiny_p = const.tile([P, 1], F32, name="tiny_p")
+        nc.vector.memset(tiny_p[:], 1e-24)
+        tiny_n = const.tile([P, 1], F32, name="tiny_n")
+        nc.vector.memset(tiny_n[:], -1e-24)
+        warm = const.tile([P, 1], F32, name="warm")
+        nc.scalar.activation(out=warm[:], in_=eps_t[:], func=ACT.Abs_reciprocal_sqrt)
+        ident = const.tile([P, P], F32, name="ident")
+        make_identity(nc, ident[:])
+        w_g = const.tile([P, 2, 512, 4], BF16, name="w_g", align_bytes=64)
+        nc.gpsimd.memset(w_g[:, :, 384:512, :], 0.0)
+        w_c = const.tile([P, 1024], U32, name="w_c", align_bytes=64)
+        w_s = const.tile([P, 1024], U8, name="w_s", align_bytes=64)
+
+        def regroup_weights(c):
+            nc.vector.tensor_copy(
+                out=w_g[:, c, 0:384, :].rearrange("p (m n) t -> p m n t", n=P),
+                in_=wraw[:, :, c, :].rearrange("p m (t n) -> p m n t", n=P),
+            )
+
+        def quant_weights():
+            nc.vector.quantize_mx(
+                out=w_c[:].bitcast(FP8X4), scales=w_s[:], in_=w_g[:].rearrange("p c n t -> p (c n t)")
+            )
+
+        def stat_cols(tau):
+            i = tau % 2
+            return (i, i + 1) if tau < 2 else (0, 2)
+
+        def sumsq(tau):
+            g, jj = divmod(tau, GROUP)
+            m, i = divmod(tau, 2)
+            if i == 0:
+                ss[m] = small.tile([P, 2], F32, name="ss")
+                rstd[m] = small.tile([P, 2], F32, name="rstd")
+            junk = junkp.tile([P, D], BF16, name="junk")
+            nc.scalar.activation(
+                out=junk[:], in_=xg[g][:, jj, :], func=ACT.Square, accum_out=ss[m][:, i : i + 1]
+            )
+
+        def rms(tau):
+            m, i = divmod(tau, 2)
+            if tau < 2 or i == 1:
+                lo, hi = stat_cols(tau)
+                nc.scalar.activation(
+                    out=rstd[m][:, lo:hi],
+                    in_=ss[m][:, lo:hi],
+                    func=ACT.Abs_reciprocal_sqrt,
+                    scale=1.0 / D,
+                    bias=eps_t[:, 0:1],
+                )
+
+        def ymul(tau):
+            g, jj = divmod(tau, GROUP)
+            m, i = divmod(tau, 2)
+            y = ypool.tile([P, 2, 4, P], F32, name="y")
+            ys[tau] = y
+            if tau > 0:
+                nc.gpsimd.tensor_scalar(
+                    out=y[:, :, :, 0:G_K],
+                    in0=xg[g][:, jj, :].rearrange("p (c k t) -> p c t k", t=4, k=P)[:, :, :, 0:G_K],
+                    scalar1=rstd[m][:, i : i + 1],
+                    scalar2=0.0,
+                    op0=ALU.mult,
+                    op1=ALU.add,
+                )
+
+        def ymul_v(tau):
+            g, jj = divmod(tau, GROUP)
+            m, i = divmod(tau, 2)
+            lo = G_K if tau > 0 else 0
+            nc.vector.tensor_scalar(
+                out=ys[tau][:, :, :, lo:P],
+                in0=xg[g][:, jj, :].rearrange("p (c k t) -> p c t k", t=4, k=P)[:, :, :, lo:P],
+                scalar1=rstd[m][:, i : i + 1],
+                scalar2=None,
+                op0=ALU.mult,
+            )
+
+        def trans(tau):
+            for c in range(2):
+                yT = ps_t.tile([P, 4, P], F32, name="yT")
+                yts[(tau, c)] = yT
+                for t in range(4):
+                    nc.tensor.transpose(out=yT[:, t, :], in_=ys[tau][:, c, t, :], identity=ident[:])
+
+        def evac(tau):
+            grp = gpool.tile([P, 1024], BF16, name="grp", align_bytes=64)
+            grps[tau] = grp
+            for c in range(2):
+                nc.vector.tensor_tensor(
+                    out=grp[:, c * 512 : (c + 1) * 512].rearrange("p (k t) -> p k t", t=4),
+                    in0=yts[(tau, c)][:].rearrange("p t k -> p k t"),
+                    in1=w4[:, c, :].unsqueeze(1).to_broadcast([P, P, 4]),
+                    op=ALU.mult,
+                )
+
+        def quant(tau):
+            codes = gpool.tile([P, 256], U32, name="codes", align_bytes=64)
+            scl = gpool.tile([P, 256], U8, name="scl", align_bytes=64)
+            cds[tau] = (codes, scl)
+            nc.vector.quantize_mx(out=codes[:].bitcast(FP8X4), scales=scl[:], in_=grps[tau][:])
+
+        def mx(tau):
+            po = ps_o.tile([P, 512], F32, name="po")
+            pos[tau] = po
+            codes, scl = cds[tau]
+            for c in range(2):
+                nc.tensor.matmul_mx(
+                    out=po[:],
+                    lhsT=codes[:, c * P : (c + 1) * P].bitcast(FP8X4),
+                    lhsT_scale=scl[:, c * P : (c + 1) * P],
+                    rhs=w_c[:, c * 512 : (c + 1) * 512].bitcast(FP8X4),
+                    rhs_scale=w_s[:, c * 512 : (c + 1) * 512],
+                    start=(c == 0),
+                    stop=(c == 1),
+                )
+
+        def heads(tau):
+            m, i = divmod(tau, 2)
+            g, jj = divmod(tau, GROUP)
+            if i == 0:
+                ssqs[m] = small.tile([P, 8], F32, name="ssq")
+            if jj == 0:
+                otile[g] = opool.tile([P, 6, GROUP, HD], F32, name="otile")
+            for w in range(4):
+                junk2 = junkp.tile([P, HD], BF16, name="junk2")
+                nc.scalar.activation(
+                    out=junk2[:],
+                    in_=pos[tau][:, w * HD : (w + 1) * HD],
+                    func=ACT.Square,
+                    accum_out=ssqs[m][:, i * 4 + w : i * 4 + w + 1],
+                )
+            nc.scalar.copy(
+                out=otile[g][:, 4:6, jj, :], in_=pos[tau][:, 256:384].rearrange("p (w d) -> p w d", d=HD)
+            )
+
+        nrm_in = {}
+
+        def clamp(m):
+            nrm_in[m] = small.tile([P, 8], F32, name="ssc")
+            nc.scalar.activation(out=nrm_in[m][:], in_=ssqs[m][:], func=ACT.Relu, bias=tiny_n[:, 0:1])
+
+        def root(m):
+            rns[m] = small.tile([P, 8], F32, name="rn")
+            nc.scalar.activation(
+                out=rns[m][:], in_=nrm_in[m][:], func=ACT.Abs_reciprocal_sqrt, bias=tiny_p[:, 0:1]
+            )
+
+        def scale(tau):
+            m, i = divmod(tau, 2)
+            g, jj = divmod(tau, GROUP)
+            nc.vector.tensor_tensor(
+                out=otile[g][:, 0:4, jj, :],
+                in0=pos[tau][:, 0:256].rearrange("p (w d) -> p w d", d=HD),
+                in1=rns[m][:, i * 4 : (i + 1) * 4].unsqueeze(2).to_broadcast([P, 4, HD]),
+                op=ALU.mult,
+            )
+
+        def store(g, lo, hi):
+            b, j0 = divmod(g * GROUP, J)
+            for m in range(3):
+                nc.sync.dma_start(
+                    out=ov[m][b][:, :, j0 + lo : j0 + hi, :], in_=otile[g][:, 2 * m : 2 * m + 2, lo:hi, :]
+                )
+
+        def ok(tau):
+            return 0 <= tau < N_TILES
+
+        for n in range(-LOAD_LEAD, N_TILES + 5):
+            if (n + LOAD_LEAD) % GROUP == 0 and 0 < (n + LOAD_LEAD) // GROUP < N_GROUPS:
+                load((n + LOAD_LEAD) // GROUP)
+            if ok(n + Y_LEAD):
+                ymul(n + Y_LEAD)
+            if ok(n + 1):
+                trans(n + 1)
+            if ok(n - 1):
+                mx(n - 1)
+            pair_done = ok(n - 2) and (n - 2) % 2 == 1
+            if ok(n - 2):
+                heads(n - 2)
+            if pair_done:
+                clamp((n - 2) // 2)
+            if ok(n + SUMSQ_LEAD - 1):
+                rms(n + SUMSQ_LEAD - 1)
+            if ok(n + SUMSQ_LEAD):
+                sumsq(n + SUMSQ_LEAD)
+            if pair_done:
+                root((n - 2) // 2)
+            if ok(n):
+                evac(n)
+            if n == 0:
+                quant_weights()
+            if ok(n - 4):
+                scale(n - 4)
+            if ok(n):
+                quant(n)
+            if ok(n + Y_LEAD):
+                ymul_v(n + Y_LEAD)
+            if n + SUMSQ_LEAD - 2 in (0, 1):
+                regroup_weights(n + SUMSQ_LEAD - 2)
+            if ok(n - 4):
+                g_out, j_out = divmod(n - 4, GROUP)
+                if g_out < N_GROUPS - 1:
+                    if j_out == GROUP - 1:
+                        store(g_out, 0, GROUP)
+                elif j_out % 2 == 1:
+                    store(g_out, j_out - 1, j_out + 1)

@@ -17,23 +17,21 @@ HD = 64
 J = L // P
 GROUP = 4
 N_TILES = B * J
+N_PAIRS = N_TILES // 2
 N_GROUPS = N_TILES // GROUP
 FLOPS = 2 * B * L * D * 384
 
-LOAD_LEAD = 11
-SUMSQ_LEAD = 7
-Y_LEAD = 3
-G_K = 88
+X_BUFS = 4
 
 
 def tile_sharedglobalattention_pa_t_kernel(tc, x, norm_w, Wq, Wk, Wv, out_0, out_1, out_2):
     nc = tc.nc
     with ExitStack() as ctx:
         const = ctx.enter_context(tc.tile_pool(name="const", bufs=1))
-        xpool = ctx.enter_context(tc.tile_pool(name="xin", bufs=4))
+        xpool = ctx.enter_context(tc.tile_pool(name="xin", bufs=X_BUFS))
         junkp = ctx.enter_context(tc.tile_pool(name="junk", bufs=2))
         small = ctx.enter_context(tc.tile_pool(name="small", bufs=8))
-        ypool = ctx.enter_context(tc.tile_pool(name="ytok", bufs=5))
+        ypool = ctx.enter_context(tc.tile_pool(name="ytok", bufs=3))
         gpool = ctx.enter_context(tc.tile_pool(name="grouped", bufs=3))
         opool = ctx.enter_context(tc.tile_pool(name="outs", bufs=3))
         ps_t = ctx.enter_context(tc.psum_pool(name="ps_t", bufs=4))
@@ -44,7 +42,7 @@ def tile_sharedglobalattention_pa_t_kernel(tc, x, norm_w, Wq, Wk, Wv, out_0, out
         outs = (out_0, out_1, out_2)
         ov = [[o[b].rearrange("n (p j) d -> p n j d", j=J) for b in range(B)] for o in outs]
 
-        xg, ss, rstd, ys, yts, grps, cds, pos, ssqs, rns, otile = {}, {}, {}, {}, {}, {}, {}, {}, {}, {}, {}
+        xg, ss, rstd, ys, yts, grps, cds, pos, ssqs, nrm_in, rns, otile = ({} for k in range(12))
 
         w4 = const.tile([P, 2, 4], BF16, name="w4")
 
@@ -60,7 +58,8 @@ def tile_sharedglobalattention_pa_t_kernel(tc, x, norm_w, Wq, Wk, Wv, out_0, out
             else:
                 nc.sync.dma_start(out=t[:], in_=xv[b][:, j0 : j0 + GROUP, :])
 
-        load(0)
+        for g in range(X_BUFS):
+            load(g)
 
         wraw = const.tile([P, 3, 2, 512], BF16, name="wraw")
         for m, w in enumerate((Wq, Wk, Wv)):
@@ -91,102 +90,88 @@ def tile_sharedglobalattention_pa_t_kernel(tc, x, norm_w, Wq, Wk, Wv, out_0, out
                 out=w_c[:].bitcast(FP8X4), scales=w_s[:], in_=w_g[:].rearrange("p c n t -> p (c n t)")
             )
 
-        def stat_cols(tau):
-            i = tau % 2
-            return (i, i + 1) if tau < 2 else (0, 2)
+        def x_tile(m, i):
+            g, jj = divmod(2 * m + i, GROUP)
+            return xg[g][:, jj, :]
 
-        def sumsq(tau):
-            g, jj = divmod(tau, GROUP)
-            m, i = divmod(tau, 2)
+        def sumsq(m, i):
             if i == 0:
                 ss[m] = small.tile([P, 2], F32, name="ss")
                 rstd[m] = small.tile([P, 2], F32, name="rstd")
             junk = junkp.tile([P, D], BF16, name="junk")
+            nc.scalar.activation(out=junk[:], in_=x_tile(m, i), func=ACT.Square, accum_out=ss[m][:, i : i + 1])
+
+        def rms(m, lo, hi):
             nc.scalar.activation(
-                out=junk[:], in_=xg[g][:, jj, :], func=ACT.Square, accum_out=ss[m][:, i : i + 1]
+                out=rstd[m][:, lo:hi],
+                in_=ss[m][:, lo:hi],
+                func=ACT.Abs_reciprocal_sqrt,
+                scale=1.0 / D,
+                bias=eps_t[:, 0:1],
             )
 
-        def rms(tau):
-            m, i = divmod(tau, 2)
-            if tau < 2 or i == 1:
-                lo, hi = stat_cols(tau)
-                nc.scalar.activation(
-                    out=rstd[m][:, lo:hi],
-                    in_=ss[m][:, lo:hi],
-                    func=ACT.Abs_reciprocal_sqrt,
-                    scale=1.0 / D,
-                    bias=eps_t[:, 0:1],
+        def ymul(m, i, on_vector=False):
+            if i == 0:
+                ys[m] = ypool.tile([P, 2, 2, 4, P], F32, name="y", align_bytes=64)
+            src = x_tile(m, i).rearrange("p (c k t) -> p c t k", t=4, k=P)
+            if on_vector:
+                nc.vector.tensor_scalar(
+                    out=ys[m][:, i], in0=src, scalar1=rstd[m][:, i : i + 1], scalar2=None, op0=ALU.mult
                 )
-
-        def ymul(tau):
-            g, jj = divmod(tau, GROUP)
-            m, i = divmod(tau, 2)
-            y = ypool.tile([P, 2, 4, P], F32, name="y")
-            ys[tau] = y
-            if tau > 0:
+            else:
                 nc.gpsimd.tensor_scalar(
-                    out=y[:, :, :, 0:G_K],
-                    in0=xg[g][:, jj, :].rearrange("p (c k t) -> p c t k", t=4, k=P)[:, :, :, 0:G_K],
+                    out=ys[m][:, i],
+                    in0=src,
                     scalar1=rstd[m][:, i : i + 1],
                     scalar2=0.0,
                     op0=ALU.mult,
                     op1=ALU.add,
                 )
 
-        def ymul_v(tau):
-            g, jj = divmod(tau, GROUP)
-            m, i = divmod(tau, 2)
-            lo = G_K if tau > 0 else 0
-            nc.vector.tensor_scalar(
-                out=ys[tau][:, :, :, lo:P],
-                in0=xg[g][:, jj, :].rearrange("p (c k t) -> p c t k", t=4, k=P)[:, :, :, lo:P],
-                scalar1=rstd[m][:, i : i + 1],
-                scalar2=None,
-                op0=ALU.mult,
-            )
-
-        def trans(tau):
+        def trans(m, i):
             for c in range(2):
                 yT = ps_t.tile([P, 4, P], F32, name="yT")
-                yts[(tau, c)] = yT
+                yts[(m, i, c)] = yT
                 for t in range(4):
-                    nc.tensor.transpose(out=yT[:, t, :], in_=ys[tau][:, c, t, :], identity=ident[:])
+                    nc.tensor.transpose(out=yT[:, t, :], in_=ys[m][:, i, c, t, :], identity=ident[:])
 
-        def evac(tau):
-            grp = gpool.tile([P, 1024], BF16, name="grp", align_bytes=64)
-            grps[tau] = grp
+        def grouped(m):
+            return ys[m][:, 0].rearrange("p c t k -> p (c t k)").bitcast(BF16)
+
+        def evac(m, i):
             for c in range(2):
+                lo = (2 * i + c) * 512
                 nc.vector.tensor_tensor(
-                    out=grp[:, c * 512 : (c + 1) * 512].rearrange("p (k t) -> p k t", t=4),
-                    in0=yts[(tau, c)][:].rearrange("p t k -> p k t"),
+                    out=grouped(m)[:, lo : lo + 512].rearrange("p (k t) -> p k t", t=4),
+                    in0=yts[(m, i, c)][:].rearrange("p t k -> p k t"),
                     in1=w4[:, c, :].unsqueeze(1).to_broadcast([P, P, 4]),
                     op=ALU.mult,
                 )
 
-        def quant(tau):
-            codes = gpool.tile([P, 256], U32, name="codes", align_bytes=64)
-            scl = gpool.tile([P, 256], U8, name="scl", align_bytes=64)
-            cds[tau] = (codes, scl)
-            nc.vector.quantize_mx(out=codes[:].bitcast(FP8X4), scales=scl[:], in_=grps[tau][:])
+        def quant(m):
+            codes = gpool.tile([P, 512], U32, name="codes", align_bytes=64)
+            scl = gpool.tile([P, 512], U8, name="scl", align_bytes=64)
+            cds[m] = (codes, scl)
+            nc.vector.quantize_mx(out=codes[:].bitcast(FP8X4), scales=scl[:], in_=grouped(m))
 
-        def mx(tau):
+        def mx(m, i):
             po = ps_o.tile([P, 512], F32, name="po")
-            pos[tau] = po
-            codes, scl = cds[tau]
+            pos[(m, i)] = po
+            codes, scl = cds[m]
             for c in range(2):
+                lo = (2 * i + c) * P
                 nc.tensor.matmul_mx(
                     out=po[:],
-                    lhsT=codes[:, c * P : (c + 1) * P].bitcast(FP8X4),
-                    lhsT_scale=scl[:, c * P : (c + 1) * P],
+                    lhsT=codes[:, lo : lo + P].bitcast(FP8X4),
+                    lhsT_scale=scl[:, lo : lo + P],
                     rhs=w_c[:, c * 512 : (c + 1) * 512].bitcast(FP8X4),
                     rhs_scale=w_s[:, c * 512 : (c + 1) * 512],
                     start=(c == 0),
                     stop=(c == 1),
                 )
 
-        def heads(tau):
-            m, i = divmod(tau, 2)
-            g, jj = divmod(tau, GROUP)
+        def heads(m, i):
+            g, jj = divmod(2 * m + i, GROUP)
             if i == 0:
                 ssqs[m] = small.tile([P, 8], F32, name="ssq")
             if jj == 0:
@@ -195,32 +180,33 @@ def tile_sharedglobalattention_pa_t_kernel(tc, x, norm_w, Wq, Wk, Wv, out_0, out
                 junk2 = junkp.tile([P, HD], BF16, name="junk2")
                 nc.scalar.activation(
                     out=junk2[:],
-                    in_=pos[tau][:, w * HD : (w + 1) * HD],
+                    in_=pos[(m, i)][:, w * HD : (w + 1) * HD],
                     func=ACT.Square,
                     accum_out=ssqs[m][:, i * 4 + w : i * 4 + w + 1],
                 )
             nc.scalar.copy(
-                out=otile[g][:, 4:6, jj, :], in_=pos[tau][:, 256:384].rearrange("p (w d) -> p w d", d=HD)
+                out=otile[g][:, 4:6, jj, :], in_=pos[(m, i)][:, 256:384].rearrange("p (w d) -> p w d", d=HD)
             )
 
-        nrm_in = {}
-
-        def clamp(m):
-            nrm_in[m] = small.tile([P, 8], F32, name="ssc")
-            nc.scalar.activation(out=nrm_in[m][:], in_=ssqs[m][:], func=ACT.Relu, bias=tiny_n[:, 0:1])
-
-        def root(m):
-            rns[m] = small.tile([P, 8], F32, name="rn")
+        def clamp(m, lo=0, hi=8):
+            if lo == 0:
+                nrm_in[m] = small.tile([P, 8], F32, name="ssc")
             nc.scalar.activation(
-                out=rns[m][:], in_=nrm_in[m][:], func=ACT.Abs_reciprocal_sqrt, bias=tiny_p[:, 0:1]
+                out=nrm_in[m][:, lo:hi], in_=ssqs[m][:, lo:hi], func=ACT.Relu, bias=tiny_n[:, 0:1]
             )
 
-        def scale(tau):
-            m, i = divmod(tau, 2)
-            g, jj = divmod(tau, GROUP)
+        def root(m, lo=0, hi=8):
+            if lo == 0:
+                rns[m] = small.tile([P, 8], F32, name="rn")
+            nc.scalar.activation(
+                out=rns[m][:, lo:hi], in_=nrm_in[m][:, lo:hi], func=ACT.Abs_reciprocal_sqrt, bias=tiny_p[:, 0:1]
+            )
+
+        def scale(m, i):
+            g, jj = divmod(2 * m + i, GROUP)
             nc.vector.tensor_tensor(
                 out=otile[g][:, 0:4, jj, :],
-                in0=pos[tau][:, 0:256].rearrange("p (w d) -> p w d", d=HD),
+                in0=pos[(m, i)][:, 0:256].rearrange("p (w d) -> p w d", d=HD),
                 in1=rns[m][:, i * 4 : (i + 1) * 4].unsqueeze(2).to_broadcast([P, 4, HD]),
                 op=ALU.mult,
             )
@@ -232,45 +218,57 @@ def tile_sharedglobalattention_pa_t_kernel(tc, x, norm_w, Wq, Wk, Wv, out_0, out
                     out=ov[m][b][:, :, j0 + lo : j0 + hi, :], in_=otile[g][:, 2 * m : 2 * m + 2, lo:hi, :]
                 )
 
-        def ok(tau):
-            return 0 <= tau < N_TILES
+        def ok(m):
+            return 0 <= m < N_PAIRS
 
-        for n in range(-LOAD_LEAD, N_TILES + 5):
-            if (n + LOAD_LEAD) % GROUP == 0 and 0 < (n + LOAD_LEAD) // GROUP < N_GROUPS:
-                load((n + LOAD_LEAD) // GROUP)
-            if ok(n + Y_LEAD):
-                ymul(n + Y_LEAD)
-            if ok(n + 1):
-                trans(n + 1)
+        for n in range(-4, N_PAIRS + 1):
+            if n >= 0 and n % 2 == 0 and n // 2 + X_BUFS < N_GROUPS:
+                load(n // 2 + X_BUFS)
             if ok(n - 1):
-                mx(n - 1)
-            pair_done = ok(n - 2) and (n - 2) % 2 == 1
-            if ok(n - 2):
-                heads(n - 2)
-            if pair_done:
-                clamp((n - 2) // 2)
-            if ok(n + SUMSQ_LEAD - 1):
-                rms(n + SUMSQ_LEAD - 1)
-            if ok(n + SUMSQ_LEAD):
-                sumsq(n + SUMSQ_LEAD)
-            if pair_done:
-                root((n - 2) // 2)
-            if ok(n):
-                evac(n)
-            if n == 0:
-                quant_weights()
-            if ok(n - 4):
-                scale(n - 4)
+                heads(n - 1, 1)
+                clamp(n - 1)
+            if ok(n + 3) and n + 3 > 0:
+                rms(n + 3, 0, 2)
+            if ok(n - 1):
+                root(n - 1)
             if ok(n):
                 quant(n)
-            if ok(n + Y_LEAD):
-                ymul_v(n + Y_LEAD)
-            if n + SUMSQ_LEAD - 2 in (0, 1):
-                regroup_weights(n + SUMSQ_LEAD - 2)
-            if ok(n - 4):
-                g_out, j_out = divmod(n - 4, GROUP)
-                if g_out < N_GROUPS - 1:
-                    if j_out == GROUP - 1:
-                        store(g_out, 0, GROUP)
-                elif j_out % 2 == 1:
-                    store(g_out, j_out - 1, j_out + 1)
+            if n == 0:
+                quant_weights()
+            if ok(n + 3):
+                ymul(n + 3, 0, on_vector=(n + 3 == 0))
+                ymul(n + 3, 1)
+            if n == -3:
+                regroup_weights(0)
+            if ok(n):
+                mx(n, 0)
+            if ok(n + 4):
+                sumsq(n + 4, 0)
+                if n + 4 == 0:
+                    rms(0, 0, 1)
+            if ok(n + 1):
+                evac(n + 1, 0)
+            if n == -1:
+                regroup_weights(1)
+            if ok(n + 2):
+                trans(n + 2, 0)
+            if ok(n - 1):
+                scale(n - 1, 0)
+            if ok(n):
+                mx(n, 1)
+                heads(n, 0)
+            if ok(n + 4):
+                sumsq(n + 4, 1)
+                if n + 4 == 0:
+                    rms(0, 1, 2)
+            if ok(n + 1):
+                evac(n + 1, 1)
+            if ok(n + 2):
+                trans(n + 2, 1)
+            if ok(n - 1):
+                scale(n - 1, 1)
+                g_out, odd = divmod(n - 1, 2)
+                if g_out == N_GROUPS - 1:
+                    store(g_out, 2 * odd, 2 * odd + 2)
+                elif odd:
+                    store(g_out, 0, GROUP)

@@ -22,6 +22,7 @@ N_GROUPS = N_TILES // GROUP
 FLOPS = 2 * B * L * D * 384
 
 X_BUFS = 4
+WARM_COLS = 256
 
 
 def tile_sharedglobalattention_pa_t_kernel(tc, x, norm_w, Wq, Wk, Wv, out_0, out_1, out_2):
@@ -74,6 +75,8 @@ def tile_sharedglobalattention_pa_t_kernel(tc, x, norm_w, Wq, Wk, Wv, out_0, out
         nc.scalar.activation(out=warm[:], in_=eps_t[:], func=ACT.Abs_reciprocal_sqrt)
         ident = const.tile([P, P], F32, name="ident")
         make_identity(nc, ident[:])
+        filler = const.tile([P, WARM_COLS], BF16, name="filler")
+        nc.vector.memset(filler[:], 0.0)
         w_g = const.tile([P, 2, 512, 4], BF16, name="w_g", align_bytes=64)
         nc.gpsimd.memset(w_g[:, :, 384:512, :], 0.0)
         w_c = const.tile([P, 1024], U32, name="w_c", align_bytes=64)
@@ -158,6 +161,7 @@ def tile_sharedglobalattention_pa_t_kernel(tc, x, norm_w, Wq, Wk, Wv, out_0, out
             po = ps_o.tile([P, 512], F32, name="po")
             pos[(m, i)] = po
             codes, scl = cds[m]
+            nc.tensor.matmul(out=po[:, 0:WARM_COLS], lhsT=filler[:, 0:P], rhs=filler[:], start=True, stop=True)
             for c in range(2):
                 lo = (2 * i + c) * P
                 nc.tensor.matmul_mx(

@@ -230,11 +230,8 @@ def tile_sharedglobalattention_pa_t_kernel(tc, x, norm_w, Wq, Wk, Wv, out_0, out
                 load(n // 2 + X_BUFS)
             if ok(n - 1):
                 heads(n - 1, 1)
-                clamp(n - 1)
             if ok(n + 3) and n + 3 > 0:
                 rms(n + 3, 0, 2)
-            if ok(n - 1):
-                root(n - 1)
             if ok(n):
                 quant(n)
             if n == 0:
@@ -250,17 +247,19 @@ def tile_sharedglobalattention_pa_t_kernel(tc, x, norm_w, Wq, Wk, Wv, out_0, out
                 sumsq(n + 4, 0)
                 if n + 4 == 0:
                     rms(0, 0, 1)
+            if ok(n - 1):
+                clamp(n - 1)
             if ok(n + 1):
                 evac(n + 1, 0)
             if n == -1:
                 regroup_weights(1)
             if ok(n + 2):
                 trans(n + 2, 0)
-            if ok(n - 1):
-                scale(n - 1, 0)
             if ok(n):
                 mx(n, 1)
                 heads(n, 0)
+            if ok(n - 1):
+                root(n - 1)
             if ok(n + 4):
                 sumsq(n + 4, 1)
                 if n + 4 == 0:
@@ -270,6 +269,7 @@ def tile_sharedglobalattention_pa_t_kernel(tc, x, norm_w, Wq, Wk, Wv, out_0, out
             if ok(n + 2):
                 trans(n + 2, 1)
             if ok(n - 1):
+                scale(n - 1, 0)
                 scale(n - 1, 1)
                 g_out, odd = divmod(n - 1, 2)
                 if g_out == N_GROUPS - 1:

@@ -22,6 +22,7 @@ N_GROUPS = N_TILES // GROUP
 FLOPS = 2 * B * L * D * 384
 
 X_BUFS = 4
+RN_SLOTS = 3
 WARM_COLS = 256
 
 
@@ -43,7 +44,7 @@ def tile_sharedglobalattention_pa_t_kernel(tc, x, norm_w, Wq, Wk, Wv, out_0, out
         outs = (out_0, out_1, out_2)
         ov = [[o[b].rearrange("n (p j) d -> p n j d", j=J) for b in range(B)] for o in outs]
 
-        xg, ss, rstd, ys, yts, grps, cds, pos, ssqs, nrm_in, rns, otile = ({} for k in range(12))
+        xg, ss, rstd, ys, yts, grps, cds, pos, ssqs, nrm_in, otile = ({} for k in range(11))
 
         w4 = const.tile([P, 2, 4], BF16, name="w4")
 
@@ -75,6 +76,8 @@ def tile_sharedglobalattention_pa_t_kernel(tc, x, norm_w, Wq, Wk, Wv, out_0, out
         nc.scalar.activation(out=warm[:], in_=eps_t[:], func=ACT.Abs_reciprocal_sqrt)
         ident = const.tile([P, P], F32, name="ident")
         make_identity(nc, ident[:])
+        rn = const.tile([P, RN_SLOTS, 2, 6], F32, name="rn")
+        nc.vector.memset(rn[:], 1.0)
         filler = const.tile([P, WARM_COLS], BF16, name="filler")
         nc.vector.memset(filler[:], 0.0)
         w_g = const.tile([P, 2, 512, 4], BF16, name="w_g", align_bytes=64)
@@ -188,30 +191,30 @@ def tile_sharedglobalattention_pa_t_kernel(tc, x, norm_w, Wq, Wk, Wv, out_0, out
                     func=ACT.Square,
                     accum_out=ssqs[m][:, i * 4 + w : i * 4 + w + 1],
                 )
-            nc.scalar.copy(
-                out=otile[g][:, 4:6, jj, :], in_=pos[(m, i)][:, 256:384].rearrange("p (w d) -> p w d", d=HD)
-            )
+            if i == 1:
+                nc.scalar.copy(
+                    out=otile[g][:, 4:6, jj, :], in_=pos[(m, i)][:, 256:384].rearrange("p (w d) -> p w d", d=HD)
+                )
 
-        def clamp(m, lo=0, hi=8):
-            if lo == 0:
-                nrm_in[m] = small.tile([P, 8], F32, name="ssc")
-            nc.scalar.activation(
-                out=nrm_in[m][:, lo:hi], in_=ssqs[m][:, lo:hi], func=ACT.Relu, bias=tiny_n[:, 0:1]
-            )
+        def clamp(m):
+            nrm_in[m] = small.tile([P, 8], F32, name="ssc")
+            nc.scalar.activation(out=nrm_in[m][:], in_=ssqs[m][:], func=ACT.Relu, bias=tiny_n[:, 0:1])
 
-        def root(m, lo=0, hi=8):
-            if lo == 0:
-                rns[m] = small.tile([P, 8], F32, name="rn")
+        def root(m):
             nc.scalar.activation(
-                out=rns[m][:, lo:hi], in_=nrm_in[m][:, lo:hi], func=ACT.Abs_reciprocal_sqrt, bias=tiny_p[:, 0:1]
+                out=rn[:, m % RN_SLOTS, :, 0:4],
+                in_=nrm_in[m][:].rearrange("p (i w) -> p i w", w=4),
+                func=ACT.Abs_reciprocal_sqrt,
+                bias=tiny_p[:, 0:1],
             )
 
         def scale(m, i):
             g, jj = divmod(2 * m + i, GROUP)
+            h = 6 if i == 0 else 4
             nc.vector.tensor_tensor(
-                out=otile[g][:, 0:4, jj, :],
-                in0=pos[(m, i)][:, 0:256].rearrange("p (w d) -> p w d", d=HD),
-                in1=rns[m][:, i * 4 : (i + 1) * 4].unsqueeze(2).to_broadcast([P, 4, HD]),
+                out=otile[g][:, 0:h, jj, :],
+                in0=pos[(m, i)][:, 0 : h * HD].rearrange("p (w d) -> p w d", d=HD),
+                in1=rn[:, m % RN_SLOTS, i, 0:h].unsqueeze(2).to_broadcast([P, h, HD]),
                 op=ALU.mult,
             )
 
@@ -232,6 +235,8 @@ def tile_sharedglobalattention_pa_t_kernel(tc, x, norm_w, Wq, Wk, Wv, out_0, out
                 heads(n - 1, 1)
             if ok(n + 3) and n + 3 > 0:
                 rms(n + 3, 0, 2)
+            if ok(n - 1):
+                clamp(n - 1)
             if ok(n):
                 quant(n)
             if n == 0:
@@ -248,7 +253,7 @@ def tile_sharedglobalattention_pa_t_kernel(tc, x, norm_w, Wq, Wk, Wv, out_0, out
                 if n + 4 == 0:
                     rms(0, 0, 1)
             if ok(n - 1):
-                clamp(n - 1)
+                root(n - 1)
             if ok(n + 1):
                 evac(n + 1, 0)
             if n == -1:
@@ -258,8 +263,6 @@ def tile_sharedglobalattention_pa_t_kernel(tc, x, norm_w, Wq, Wk, Wv, out_0, out
             if ok(n):
                 mx(n, 1)
                 heads(n, 0)
-            if ok(n - 1):
-                root(n - 1)
             if ok(n + 4):
                 sumsq(n + 4, 1)
                 if n + 4 == 0:

@@ -142,9 +142,11 @@ def tile_sharedglobalattention_pa_t_kernel(tc, x, norm_w, Wq, Wk, Wv, out_0, out
                     nc.tensor.transpose(out=yT[:, t, :], in_=ys[m][:, i, c, t, :], identity=ident[:])
 
         def grouped(m):
-            return ys[m][:, 0].rearrange("p c t k -> p (c t k)").bitcast(BF16)
+            return grps[m][:]
 
         def evac(m, i):
+            if i == 0:
+                grps[m] = gpool.tile([P, 2048], BF16, name="grp", align_bytes=64)
             for c in range(2):
                 lo = (2 * i + c) * 512
                 nc.vector.tensor_tensor(

@@ -193,10 +193,6 @@ def tile_sharedglobalattention_pa_t_kernel(tc, x, norm_w, Wq, Wk, Wv, out_0, out
                     func=ACT.Square,
                     accum_out=ssqs[m][:, i * 4 + w : i * 4 + w + 1],
                 )
-            if i == 1:
-                nc.scalar.copy(
-                    out=otile[g][:, 4:6, jj, :], in_=pos[(m, i)][:, 256:384].rearrange("p (w d) -> p w d", d=HD)
-                )
 
         def clamp(m):
             nrm_in[m] = small.tile([P, 8], F32, name="ssc")
@@ -212,11 +208,10 @@ def tile_sharedglobalattention_pa_t_kernel(tc, x, norm_w, Wq, Wk, Wv, out_0, out
 
         def scale(m, i):
             g, jj = divmod(2 * m + i, GROUP)
-            h = 6 if i == 0 else 4
             nc.vector.tensor_tensor(
-                out=otile[g][:, 0:h, jj, :],
-                in0=pos[(m, i)][:, 0 : h * HD].rearrange("p (w d) -> p w d", d=HD),
-                in1=rn[:, m % RN_SLOTS, i, 0:h].unsqueeze(2).to_broadcast([P, h, HD]),
+                out=otile[g][:, :, jj, :],
+                in0=pos[(m, i)][:, 0:384].rearrange("p (w d) -> p w d", d=HD),
+                in1=rn[:, m % RN_SLOTS, i, :].unsqueeze(2).to_broadcast([P, 6, HD]),
                 op=ALU.mult,
             )
 

@@ -19,10 +19,13 @@ GROUP = 4
 N_TILES = B * J
 N_PAIRS = N_TILES // 2
 N_GROUPS = N_TILES // GROUP
+LASTP = N_PAIRS - 1
 FLOPS = 2 * B * L * D * 384
 
 X_BUFS = 4
 RN_SLOTS = 3
+ONE_BY_ONE = 3
+V_TO = 28
 WARM_COLS = 256
 
 
@@ -31,7 +34,7 @@ def tile_sharedglobalattention_pa_t_kernel(tc, x, norm_w, Wq, Wk, Wv, out_0, out
     with ExitStack() as ctx:
         const = ctx.enter_context(tc.tile_pool(name="const", bufs=1))
         xpool = ctx.enter_context(tc.tile_pool(name="xin", bufs=X_BUFS))
-        junkp = ctx.enter_context(tc.tile_pool(name="junk", bufs=2))
+        junkp = ctx.enter_context(tc.tile_pool(name="junk", bufs=8))
         small = ctx.enter_context(tc.tile_pool(name="small", bufs=8))
         ypool = ctx.enter_context(tc.tile_pool(name="ytok", bufs=3))
         gpool = ctx.enter_context(tc.tile_pool(name="grouped", bufs=3))
@@ -47,6 +50,7 @@ def tile_sharedglobalattention_pa_t_kernel(tc, x, norm_w, Wq, Wk, Wv, out_0, out
         xg, ss, rstd, ys, yts, grps, cds, pos, ssqs, nrm_in, otile = ({} for k in range(11))
 
         w4 = const.tile([P, 2, 4], BF16, name="w4")
+        wraw = const.tile([P, 3, 2, 512], BF16, name="wraw")
 
         def load(g):
             b, j0 = divmod(g * GROUP, J)
@@ -57,15 +61,17 @@ def tile_sharedglobalattention_pa_t_kernel(tc, x, norm_w, Wq, Wk, Wv, out_0, out
                     nc.sync.dma_start(out=t[:, jj : jj + 1, :], in_=xv[b][:, j0 + jj : j0 + jj + 1, :])
                     if jj == 0:
                         nc.sync.dma_start(out=w4[:], in_=norm_w.rearrange("(c p t) -> p c t", p=P, t=4))
+                        for c in range(2):
+                            for m, w in enumerate((Wq, Wk, Wv)):
+                                nc.sync.dma_start(
+                                    out=wraw[:, m, c, :], in_=w.rearrange("(c p t) n -> c p (t n)", p=P, t=4)[c]
+                                )
             else:
                 nc.sync.dma_start(out=t[:], in_=xv[b][:, j0 : j0 + GROUP, :])
 
         for g in range(X_BUFS):
             load(g)
 
-        wraw = const.tile([P, 3, 2, 512], BF16, name="wraw")
-        for m, w in enumerate((Wq, Wk, Wv)):
-            nc.scalar.dma_start(out=wraw[:, m], in_=w.rearrange("(c p t) n -> p c (t n)", p=P, t=4))
         eps_t = const.tile([P, 1], F32, name="eps_t")
         nc.vector.memset(eps_t[:], 1e-6)
         tiny_p = const.tile([P, 1], F32, name="tiny_p")
@@ -141,26 +147,29 @@ def tile_sharedglobalattention_pa_t_kernel(tc, x, norm_w, Wq, Wk, Wv, out_0, out
                 for t in range(4):
                     nc.tensor.transpose(out=yT[:, t, :], in_=ys[m][:, i, c, t, :], identity=ident[:])
 
-        def grouped(m):
-            return grps[m][:]
-
         def evac(m, i):
             if i == 0:
                 grps[m] = gpool.tile([P, 2048], BF16, name="grp", align_bytes=64)
             for c in range(2):
                 lo = (2 * i + c) * 512
                 nc.vector.tensor_tensor(
-                    out=grouped(m)[:, lo : lo + 512].rearrange("p (k t) -> p k t", t=4),
+                    out=grps[m][:, lo : lo + 512].rearrange("p (k t) -> p k t", t=4),
                     in0=yts[(m, i, c)][:].rearrange("p t k -> p k t"),
                     in1=w4[:, c, :].unsqueeze(1).to_broadcast([P, P, 4]),
                     op=ALU.mult,
                 )
 
-        def quant(m):
-            codes = gpool.tile([P, 512], U32, name="codes", align_bytes=64)
-            scl = gpool.tile([P, 512], U8, name="scl", align_bytes=64)
-            cds[m] = (codes, scl)
-            nc.vector.quantize_mx(out=codes[:].bitcast(FP8X4), scales=scl[:], in_=grouped(m))
+        def quant(m, i=0, tiles=2):
+            if i == 0:
+                cds[m] = (
+                    gpool.tile([P, 512], U32, name="codes", align_bytes=64),
+                    gpool.tile([P, 512], U8, name="scl", align_bytes=64),
+                )
+            codes, scl = cds[m]
+            lo, hi = i * 256, (i + tiles) * 256
+            nc.vector.quantize_mx(
+                out=codes[:, lo:hi].bitcast(FP8X4), scales=scl[:, lo:hi], in_=grps[m][:, 4 * lo : 4 * hi]
+            )
 
         def mx(m, i):
             po = ps_o.tile([P, 512], F32, name="po")
@@ -179,6 +188,9 @@ def tile_sharedglobalattention_pa_t_kernel(tc, x, norm_w, Wq, Wk, Wv, out_0, out
                     stop=(c == 1),
                 )
 
+        def v_on_vector(m, i):
+            return m < V_TO
+
         def heads(m, i):
             g, jj = divmod(2 * m + i, GROUP)
             if i == 0:
@@ -193,25 +205,34 @@ def tile_sharedglobalattention_pa_t_kernel(tc, x, norm_w, Wq, Wk, Wv, out_0, out
                     func=ACT.Square,
                     accum_out=ssqs[m][:, i * 4 + w : i * 4 + w + 1],
                 )
+            if not v_on_vector(m, i):
+                nc.scalar.copy(
+                    out=otile[g][:, 4:6, jj, :], in_=pos[(m, i)][:, 256:384].rearrange("p (w d) -> p w d", d=HD)
+                )
 
-        def clamp(m):
-            nrm_in[m] = small.tile([P, 8], F32, name="ssc")
-            nc.scalar.activation(out=nrm_in[m][:], in_=ssqs[m][:], func=ACT.Relu, bias=tiny_n[:, 0:1])
-
-        def root(m):
+        def clamp(m, i=0, tiles=2):
+            if i == 0:
+                nrm_in[m] = small.tile([P, 8], F32, name="ssc")
+            lo, hi = i * 4, (i + tiles) * 4
             nc.scalar.activation(
-                out=rn[:, m % RN_SLOTS, :, 0:4],
-                in_=nrm_in[m][:].rearrange("p (i w) -> p i w", w=4),
+                out=nrm_in[m][:, lo:hi], in_=ssqs[m][:, lo:hi], func=ACT.Relu, bias=tiny_n[:, 0:1]
+            )
+
+        def root(m, i=0, tiles=2):
+            nc.scalar.activation(
+                out=rn[:, m % RN_SLOTS, i : i + tiles, 0:4],
+                in_=nrm_in[m][:, i * 4 : (i + tiles) * 4].rearrange("p (i w) -> p i w", w=4),
                 func=ACT.Abs_reciprocal_sqrt,
                 bias=tiny_p[:, 0:1],
             )
 
         def scale(m, i):
             g, jj = divmod(2 * m + i, GROUP)
+            h = 6 if v_on_vector(m, i) else 4
             nc.vector.tensor_tensor(
-                out=otile[g][:, :, jj, :],
-                in0=pos[(m, i)][:, 0:384].rearrange("p (w d) -> p w d", d=HD),
-                in1=rn[:, m % RN_SLOTS, i, :].unsqueeze(2).to_broadcast([P, 6, HD]),
+                out=otile[g][:, 0:h, jj, :],
+                in0=pos[(m, i)][:, 0 : h * HD].rearrange("p (w d) -> p w d", d=HD),
+                in1=rn[:, m % RN_SLOTS, i, 0:h].unsqueeze(2).to_broadcast([P, h, HD]),
                 op=ALU.mult,
             )
 
@@ -230,49 +251,69 @@ def tile_sharedglobalattention_pa_t_kernel(tc, x, norm_w, Wq, Wk, Wv, out_0, out
                 load(n // 2 + X_BUFS)
             if ok(n - 1):
                 heads(n - 1, 1)
-            if ok(n + 3) and n + 3 > 0:
+            if ok(n + 3) and n + 3 >= ONE_BY_ONE:
                 rms(n + 3, 0, 2)
-            if ok(n - 1):
-                clamp(n - 1)
-            if ok(n):
-                quant(n)
             if n == 0:
-                quant_weights()
+                evac(1, 0)
+            if ok(n) and n != LASTP:
+                quant(n)
+            if n == LASTP:
+                quant(n, 1, 1)
             if ok(n + 3):
+                if n + 3 == 0:
+                    regroup_weights(0)
                 ymul(n + 3, 0, on_vector=(n + 3 == 0))
-                ymul(n + 3, 1)
-            if n == -3:
-                regroup_weights(0)
-            if ok(n):
+                if n + 3 == 0:
+                    regroup_weights(1)
+                    quant_weights()
+                ymul(n + 3, 1, on_vector=(n + 3 == 0))
+            if ok(n) and n != LASTP:
                 mx(n, 0)
             if ok(n + 4):
                 sumsq(n + 4, 0)
-                if n + 4 == 0:
-                    rms(0, 0, 1)
-            if ok(n - 1):
-                root(n - 1)
-            if ok(n + 1):
+                if n + 4 < ONE_BY_ONE:
+                    rms(n + 4, 0, 1)
+            if n == N_PAIRS:
+                root(LASTP, 0, 1)
+                scale(LASTP, 0)
+                clamp(LASTP, 1, 1)
+            elif ok(n - 1):
+                clamp(n - 1)
+            if ok(n + 1) and n != 0:
                 evac(n + 1, 0)
-            if n == -1:
-                regroup_weights(1)
+            if n + 1 == LASTP:
+                quant(n + 1, 0, 1)
             if ok(n + 2):
                 trans(n + 2, 0)
             if ok(n):
                 mx(n, 1)
+            if n + 1 == LASTP:
+                mx(n + 1, 0)
+            if ok(n):
                 heads(n, 0)
+            if n == N_PAIRS:
+                root(LASTP, 1, 1)
+            elif ok(n - 1):
+                root(n - 1)
+            if n == LASTP:
+                clamp(LASTP, 0, 1)
             if ok(n + 4):
                 sumsq(n + 4, 1)
-                if n + 4 == 0:
-                    rms(0, 1, 2)
+                if n + 4 < ONE_BY_ONE:
+                    rms(n + 4, 1, 2)
             if ok(n + 1):
                 evac(n + 1, 1)
             if ok(n + 2):
                 trans(n + 2, 1)
             if ok(n - 1):
-                scale(n - 1, 0)
+                if n < N_PAIRS:
+                    scale(n - 1, 0)
                 scale(n - 1, 1)
                 g_out, odd = divmod(n - 1, 2)
-                if g_out == N_GROUPS - 1:
+                if n == N_PAIRS:
+                    store(g_out, 2, 3)
+                    store(g_out, 3, 4)
+                elif g_out == N_GROUPS - 1:
                     store(g_out, 2 * odd, 2 * odd + 2)
                 elif odd:
                     store(g_out, 0, GROUP)

@@ -24,7 +24,7 @@ FLOPS = 2 * B * L * D * 384
 
 X_BUFS = 4
 RN_SLOTS = 3
-ONE_BY_ONE = 3
+ONE_BY_ONE = 2
 V_TO = 28
 WARM_COLS = 256
 
@@ -189,7 +189,7 @@ def tile_sharedglobalattention_pa_t_kernel(tc, x, norm_w, Wq, Wk, Wv, out_0, out
                 )
 
         def v_on_vector(m, i):
-            return m < V_TO
+            return i == 0 and m < V_TO
 
         def heads(m, i):
             g, jj = divmod(2 * m + i, GROUP)
@@ -253,8 +253,6 @@ def tile_sharedglobalattention_pa_t_kernel(tc, x, norm_w, Wq, Wk, Wv, out_0, out
                 heads(n - 1, 1)
             if ok(n + 3) and n + 3 >= ONE_BY_ONE:
                 rms(n + 3, 0, 2)
-            if n == 0:
-                evac(1, 0)
             if ok(n) and n != LASTP:
                 quant(n)
             if n == LASTP:
@@ -279,7 +277,7 @@ def tile_sharedglobalattention_pa_t_kernel(tc, x, norm_w, Wq, Wk, Wv, out_0, out
                 clamp(LASTP, 1, 1)
             elif ok(n - 1):
                 clamp(n - 1)
-            if ok(n + 1) and n != 0:
+            if ok(n + 1):
                 evac(n + 1, 0)
             if n + 1 == LASTP:
                 quant(n + 1, 0, 1)

@@ -24,9 +24,10 @@ FLOPS = 2 * B * L * D * 384
 
 X_BUFS = 4
 RN_SLOTS = 3
+RMS_AT = 2
 ONE_BY_ONE = 2
 V_TO = 28
-WARM_COLS = 256
+WARM_COLS = 128
 
 
 def tile_sharedglobalattention_pa_t_kernel(tc, x, norm_w, Wq, Wk, Wv, out_0, out_1, out_2):
@@ -47,7 +48,7 @@ def tile_sharedglobalattention_pa_t_kernel(tc, x, norm_w, Wq, Wk, Wv, out_0, out
         outs = (out_0, out_1, out_2)
         ov = [[o[b].rearrange("n (p j) d -> p n j d", j=J) for b in range(B)] for o in outs]
 
-        xg, ss, rstd, ys, yts, grps, cds, pos, ssqs, nrm_in, otile = ({} for k in range(11))
+        xg, ss, rstd, ys, yts, grps, cds, pos, ssqs, otile = ({} for k in range(10))
 
         w4 = const.tile([P, 2, 4], BF16, name="w4")
         wraw = const.tile([P, 3, 2, 512], BF16, name="wraw")
@@ -74,10 +75,8 @@ def tile_sharedglobalattention_pa_t_kernel(tc, x, norm_w, Wq, Wk, Wv, out_0, out
 
         eps_t = const.tile([P, 1], F32, name="eps_t")
         nc.vector.memset(eps_t[:], 1e-6)
-        tiny_p = const.tile([P, 1], F32, name="tiny_p")
-        nc.vector.memset(tiny_p[:], 1e-24)
-        tiny_n = const.tile([P, 1], F32, name="tiny_n")
-        nc.vector.memset(tiny_n[:], -1e-24)
+        tiny = const.tile([P, 1], F32, name="tiny")
+        nc.vector.memset(tiny[:], 1e-36)
         warm = const.tile([P, 1], F32, name="warm")
         nc.scalar.activation(out=warm[:], in_=eps_t[:], func=ACT.Abs_reciprocal_sqrt)
         ident = const.tile([P, P], F32, name="ident")
@@ -188,16 +187,19 @@ def tile_sharedglobalattention_pa_t_kernel(tc, x, norm_w, Wq, Wk, Wv, out_0, out
                     stop=(c == 1),
                 )
 
-        def v_on_vector(m, i):
-            return i == 0 and m < V_TO
+        def on_scalar(m):
+            return V_TO <= m < LASTP
 
-        def heads(m, i):
+        def v_on_vector(m, i):
+            return m < V_TO and i == 0 and m % 2 == 0
+
+        def heads(m, i, lo=0, hi=4):
             g, jj = divmod(2 * m + i, GROUP)
-            if i == 0:
+            if i == 0 and lo == 0:
                 ssqs[m] = small.tile([P, 8], F32, name="ssq")
-            if jj == 0:
+            if jj == 0 and lo == 0:
                 otile[g] = opool.tile([P, 6, GROUP, HD], F32, name="otile")
-            for w in range(4):
+            for w in range(lo, hi):
                 junk2 = junkp.tile([P, HD], BF16, name="junk2")
                 nc.scalar.activation(
                     out=junk2[:],
@@ -205,35 +207,43 @@ def tile_sharedglobalattention_pa_t_kernel(tc, x, norm_w, Wq, Wk, Wv, out_0, out
                     func=ACT.Square,
                     accum_out=ssqs[m][:, i * 4 + w : i * 4 + w + 1],
                 )
-            if not v_on_vector(m, i):
+            if hi == 4 and not v_on_vector(m, i):
                 nc.scalar.copy(
                     out=otile[g][:, 4:6, jj, :], in_=pos[(m, i)][:, 256:384].rearrange("p (w d) -> p w d", d=HD)
                 )
 
-        def clamp(m, i=0, tiles=2):
-            if i == 0:
-                nrm_in[m] = small.tile([P, 8], F32, name="ssc")
-            lo, hi = i * 4, (i + tiles) * 4
-            nc.scalar.activation(
-                out=nrm_in[m][:, lo:hi], in_=ssqs[m][:, lo:hi], func=ACT.Relu, bias=tiny_n[:, 0:1]
-            )
-
         def root(m, i=0, tiles=2):
             nc.scalar.activation(
                 out=rn[:, m % RN_SLOTS, i : i + tiles, 0:4],
-                in_=nrm_in[m][:, i * 4 : (i + tiles) * 4].rearrange("p (i w) -> p i w", w=4),
+                in_=ssqs[m][:, i * 4 : (i + tiles) * 4].rearrange("p (i w) -> p i w", w=4),
                 func=ACT.Abs_reciprocal_sqrt,
-                bias=tiny_p[:, 0:1],
+                bias=tiny[:, 0:1],
             )
+
+        def clip(m, i):
+            r = rn[:, m % RN_SLOTS, i, 0:4]
+            nc.gpsimd.tensor_scalar(out=r, in0=r, scalar1=1e12, scalar2=0.0, op0=ALU.min, op1=ALU.add)
+
+        def scale_on_scalar(m, i):
+            g, jj = divmod(2 * m + i, GROUP)
+            for w in range(4):
+                nc.scalar.activation(
+                    out=otile[g][:, w, jj, :],
+                    in_=pos[(m, i)][:, w * HD : (w + 1) * HD],
+                    func=ACT.Copy,
+                    scale=rn[:, m % RN_SLOTS, i, w : w + 1],
+                )
 
         def scale(m, i):
             g, jj = divmod(2 * m + i, GROUP)
             h = 6 if v_on_vector(m, i) else 4
-            nc.vector.tensor_tensor(
+            nc.vector.scalar_tensor_tensor(
                 out=otile[g][:, 0:h, jj, :],
-                in0=pos[(m, i)][:, 0 : h * HD].rearrange("p (w d) -> p w d", d=HD),
-                in1=rn[:, m % RN_SLOTS, i, 0:h].unsqueeze(2).to_broadcast([P, h, HD]),
-                op=ALU.mult,
+                in0=rn[:, m % RN_SLOTS, i, 0:h].unsqueeze(2).to_broadcast([P, h, HD]),
+                scalar=1e12,
+                in1=pos[(m, i)][:, 0 : h * HD].rearrange("p (w d) -> p w d", d=HD),
+                op0=ALU.min,
+                op1=ALU.mult,
             )
 
         def store(g, lo, hi):
@@ -246,13 +256,22 @@ def tile_sharedglobalattention_pa_t_kernel(tc, x, norm_w, Wq, Wk, Wv, out_0, out
         def ok(m):
             return 0 <= m < N_PAIRS
 
+        def keep_warm(count):
+            wt = ps_o.tile([P, 512], F32, name="po")
+            for k in range(count):
+                nc.tensor.matmul(out=wt[:, 0:P], lhsT=ident[:], rhs=ident[:], start=True, stop=True)
+
+        keep_warm(14)
+
         for n in range(-4, N_PAIRS + 1):
             if n >= 0 and n % 2 == 0 and n // 2 + X_BUFS < N_GROUPS:
                 load(n // 2 + X_BUFS)
             if ok(n - 1):
-                heads(n - 1, 1)
+                heads(n - 1, 1, 0, RMS_AT)
             if ok(n + 3) and n + 3 >= ONE_BY_ONE:
                 rms(n + 3, 0, 2)
+            if ok(n - 1):
+                heads(n - 1, 1, RMS_AT, 4)
             if ok(n) and n != LASTP:
                 quant(n)
             if n == LASTP:
@@ -272,29 +291,32 @@ def tile_sharedglobalattention_pa_t_kernel(tc, x, norm_w, Wq, Wk, Wv, out_0, out
                 if n + 4 < ONE_BY_ONE:
                     rms(n + 4, 0, 1)
             if n == N_PAIRS:
-                root(LASTP, 0, 1)
                 scale(LASTP, 0)
-                clamp(LASTP, 1, 1)
+                root(LASTP, 1, 1)
             elif ok(n - 1):
-                clamp(n - 1)
+                root(n - 1)
+                if on_scalar(n - 1):
+                    clip(n - 1, 1)
             if ok(n + 1):
                 evac(n + 1, 0)
             if n + 1 == LASTP:
                 quant(n + 1, 0, 1)
             if ok(n + 2):
                 trans(n + 2, 0)
+            if n + 2 == 0:
+                keep_warm(5)
+            if n + 2 == 1:
+                keep_warm(2)
             if ok(n):
                 mx(n, 1)
             if n + 1 == LASTP:
                 mx(n + 1, 0)
             if ok(n):
                 heads(n, 0)
-            if n == N_PAIRS:
-                root(LASTP, 1, 1)
-            elif ok(n - 1):
-                root(n - 1)
+            if on_scalar(n - 1):
+                scale_on_scalar(n - 1, 1)
             if n == LASTP:
-                clamp(LASTP, 0, 1)
+                root(LASTP, 0, 1)
             if ok(n + 4):
                 sumsq(n + 4, 1)
                 if n + 4 < ONE_BY_ONE:
@@ -303,10 +325,15 @@ def tile_sharedglobalattention_pa_t_kernel(tc, x, norm_w, Wq, Wk, Wv, out_0, out
                 evac(n + 1, 1)
             if ok(n + 2):
                 trans(n + 2, 1)
+            if n + 2 == 0:
+                keep_warm(2)
+            if n + 2 == 1:
+                keep_warm(2)
             if ok(n - 1):
                 if n < N_PAIRS:
                     scale(n - 1, 0)
-                scale(n - 1, 1)
+                if not on_scalar(n - 1):
+                    scale(n - 1, 1)
                 g_out, odd = divmod(n - 1, 2)
                 if n == N_PAIRS:
                     store(g_out, 2, 3)

@@ -62,7 +62,8 @@ def tile_sharedglobalattention_pa_t_kernel(tc, x, norm_w, Wq, Wk, Wv, out_0, out
                     nc.sync.dma_start(out=t[:, jj : jj + 1, :], in_=xv[b][:, j0 + jj : j0 + jj + 1, :])
                     if jj == 0:
                         nc.sync.dma_start(out=w4[:], in_=norm_w.rearrange("(c p t) -> p c t", p=P, t=4))
-                        for c in range(2):
+                    for c in range(2):
+                        if jj == (0, 1)[c]:
                             for m, w in enumerate((Wq, Wk, Wv)):
                                 nc.sync.dma_start(
                                     out=wraw[:, m, c, :], in_=w.rearrange("(c p t) n -> c p (t n)", p=P, t=4)[c]
@@ -248,7 +249,7 @@ def tile_sharedglobalattention_pa_t_kernel(tc, x, norm_w, Wq, Wk, Wv, out_0, out
 
         def store(g, lo, hi):
             b, j0 = divmod(g * GROUP, J)
-            for m in range(3):
+            for m in (2, 0, 1):
                 nc.sync.dma_start(
                     out=ov[m][b][:, :, j0 + lo : j0 + hi, :], in_=otile[g][:, 2 * m : 2 * m + 2, lo:hi, :]
                 )
@@ -274,8 +275,6 @@ def tile_sharedglobalattention_pa_t_kernel(tc, x, norm_w, Wq, Wk, Wv, out_0, out
                 heads(n - 1, 1, RMS_AT, 4)
             if ok(n) and n != LASTP:
                 quant(n)
-            if n == LASTP:
-                quant(n, 1, 1)
             if ok(n + 3):
                 if n + 3 == 0:
                     regroup_weights(0)
@@ -300,6 +299,7 @@ def tile_sharedglobalattention_pa_t_kernel(tc, x, norm_w, Wq, Wk, Wv, out_0, out
             if ok(n + 1):
                 evac(n + 1, 0)
             if n + 1 == LASTP:
+                scale(n - 1, 0)
                 quant(n + 1, 0, 1)
             if ok(n + 2):
                 trans(n + 2, 0)
@@ -323,6 +323,8 @@ def tile_sharedglobalattention_pa_t_kernel(tc, x, norm_w, Wq, Wk, Wv, out_0, out
                     rms(n + 4, 1, 2)
             if ok(n + 1):
                 evac(n + 1, 1)
+            if n + 1 == LASTP:
+                quant(n + 1, 1, 1)
             if ok(n + 2):
                 trans(n + 2, 1)
             if n + 2 == 0:
@@ -330,7 +332,7 @@ def tile_sharedglobalattention_pa_t_kernel(tc, x, norm_w, Wq, Wk, Wv, out_0, out
             if n + 2 == 1:
                 keep_warm(2)
             if ok(n - 1):
-                if n < N_PAIRS:
+                if n + 1 != LASTP and n != N_PAIRS:
                     scale(n - 1, 0)
                 if not on_scalar(n - 1):
                     scale(n - 1, 1)

@@ -60,14 +60,14 @@ def tile_sharedglobalattention_pa_t_kernel(tc, x, norm_w, Wq, Wk, Wv, out_0, out
             if g == 0:
                 for jj in range(GROUP):
                     nc.sync.dma_start(out=t[:, jj : jj + 1, :], in_=xv[b][:, j0 + jj : j0 + jj + 1, :])
-                    if jj == 0:
-                        nc.sync.dma_start(out=w4[:], in_=norm_w.rearrange("(c p t) -> p c t", p=P, t=4))
                     for c in range(2):
                         if jj == (0, 1)[c]:
                             for m, w in enumerate((Wq, Wk, Wv)):
                                 nc.sync.dma_start(
                                     out=wraw[:, m, c, :], in_=w.rearrange("(c p t) n -> c p (t n)", p=P, t=4)[c]
                                 )
+                    if jj == 1:
+                        nc.sync.dma_start(out=w4[:], in_=norm_w.rearrange("(c p t) -> p c t", p=P, t=4))
             else:
                 nc.sync.dma_start(out=t[:], in_=xv[b][:, j0 : j0 + GROUP, :])
 
@@ -153,9 +153,9 @@ def tile_sharedglobalattention_pa_t_kernel(tc, x, norm_w, Wq, Wk, Wv, out_0, out
             for c in range(2):
                 lo = (2 * i + c) * 512
                 nc.vector.tensor_tensor(
-                    out=grps[m][:, lo : lo + 512].rearrange("p (k t) -> p k t", t=4),
-                    in0=yts[(m, i, c)][:].rearrange("p t k -> p k t"),
-                    in1=w4[:, c, :].unsqueeze(1).to_broadcast([P, P, 4]),
+                    out=grps[m][:, lo : lo + 512].rearrange("p (k i t) -> p k t i", i=2, t=4),
+                    in0=yts[(m, i, c)][:].rearrange("p t (k i) -> p k t i", i=2),
+                    in1=w4[:, c, :].unsqueeze(1).unsqueeze(3).to_broadcast([P, P // 2, 4, 2]),
                     op=ALU.mult,
                 )
 

from contextlib import ExitStack

import concourse.mybir as mybir
from concourse.masks import make_identity

F32 = mybir.dt.float32
BF16 = mybir.dt.bfloat16
U32 = mybir.dt.uint32
U8 = mybir.dt.uint8
FP8X4 = mybir.dt.float8_e4m3fn_x4
ACT = mybir.ActivationFunctionType
ALU = mybir.AluOpType

P = 128
B, L, D = 4, 2048, 1024
HD = 64
J = L // P
GROUP = 4
N_TILES = B * J
N_PAIRS = N_TILES // 2
N_GROUPS = N_TILES // GROUP
LASTP = N_PAIRS - 1
FLOPS = 2 * B * L * D * 384

X_BUFS = 4
RN_SLOTS = 3
RMS_AT = 2
ONE_BY_ONE = 2
V_TO = 28
WARM_COLS = 128


def tile_sharedglobalattention_pa_t_kernel(tc, x, norm_w, Wq, Wk, Wv, out_0, out_1, out_2):
    nc = tc.nc
    with ExitStack() as ctx:
        const = ctx.enter_context(tc.tile_pool(name="const", bufs=1))
        xpool = ctx.enter_context(tc.tile_pool(name="xin", bufs=X_BUFS))
        junkp = ctx.enter_context(tc.tile_pool(name="junk", bufs=8))
        small = ctx.enter_context(tc.tile_pool(name="small", bufs=8))
        ypool = ctx.enter_context(tc.tile_pool(name="ytok", bufs=3))
        gpool = ctx.enter_context(tc.tile_pool(name="grouped", bufs=3))
        opool = ctx.enter_context(tc.tile_pool(name="outs", bufs=3))
        ps_t = ctx.enter_context(tc.psum_pool(name="ps_t", bufs=4))
        ps_o = ctx.enter_context(tc.psum_pool(name="ps_o", bufs=4))
        ctx.enter_context(tc.manual_schedule())

        xv = [x[b].rearrange("(p j) d -> p j d", j=J) for b in range(B)]
        outs = (out_0, out_1, out_2)
        ov = [[o[b].rearrange("n (p j) d -> p n j d", j=J) for b in range(B)] for o in outs]

        xg, ss, rstd, ys, yts, grps, cds, pos, ssqs, otile = ({} for k in range(10))

        w4 = const.tile([P, 2, 4], BF16, name="w4")
        wraw = const.tile([P, 3, 2, 512], BF16, name="wraw")

        def load(g):
            b, j0 = divmod(g * GROUP, J)
            t = xpool.tile([P, GROUP, D], BF16, name="xg")
            xg[g] = t
            if g == 0:
                for jj in range(GROUP):
                    nc.sync.dma_start(out=t[:, jj : jj + 1, :], in_=xv[b][:, j0 + jj : j0 + jj + 1, :])
                    for c in range(2):
                        if jj == (0, 1)[c]:
                            for m, w in enumerate((Wq, Wk, Wv)):
                                nc.sync.dma_start(
                                    out=wraw[:, m, c, :], in_=w.rearrange("(c p t) n -> c p (t n)", p=P, t=4)[c]
                                )
                    if jj == 1:
                        nc.sync.dma_start(out=w4[:], in_=norm_w.rearrange("(c p t) -> p c t", p=P, t=4))
            else:
                nc.sync.dma_start(out=t[:], in_=xv[b][:, j0 : j0 + GROUP, :])

        for g in range(X_BUFS):
            load(g)

        eps_t = const.tile([P, 1], F32, name="eps_t")
        nc.vector.memset(eps_t[:], 1e-6)
        tiny = const.tile([P, 1], F32, name="tiny")
        nc.vector.memset(tiny[:], 1e-36)
        warm = const.tile([P, 1], F32, name="warm")
        nc.scalar.activation(out=warm[:], in_=eps_t[:], func=ACT.Abs_reciprocal_sqrt)
        ident = const.tile([P, P], F32, name="ident")
        make_identity(nc, ident[:])
        rn = const.tile([P, RN_SLOTS, 2, 6], F32, name="rn")
        nc.vector.memset(rn[:], 1.0)
        filler = const.tile([P, WARM_COLS], BF16, name="filler")
        nc.vector.memset(filler[:], 0.0)
        w_g = const.tile([P, 2, 512, 4], BF16, name="w_g", align_bytes=64)
        nc.gpsimd.memset(w_g[:, :, 384:512, :], 0.0)
        w_c = const.tile([P, 1024], U32, name="w_c", align_bytes=64)
        w_s = const.tile([P, 1024], U8, name="w_s", align_bytes=64)

        def regroup_weights(c):
            nc.vector.tensor_copy(
                out=w_g[:, c, 0:384, :].rearrange("p (m n) t -> p m n t", n=P),
                in_=wraw[:, :, c, :].rearrange("p m (t n) -> p m n t", n=P),
            )

        def quant_weights():
            nc.vector.quantize_mx(
                out=w_c[:].bitcast(FP8X4), scales=w_s[:], in_=w_g[:].rearrange("p c n t -> p (c n t)")
            )

        def x_tile(m, i):
            g, jj = divmod(2 * m + i, GROUP)
            return xg[g][:, jj, :]

        def sumsq(m, i):
            if i == 0:
                ss[m] = small.tile([P, 2], F32, name="ss")
                rstd[m] = small.tile([P, 2], F32, name="rstd")
            junk = junkp.tile([P, D], BF16, name="junk")
            nc.scalar.activation(out=junk[:], in_=x_tile(m, i), func=ACT.Square, accum_out=ss[m][:, i : i + 1])

        def rms(m, lo, hi):
            nc.scalar.activation(
                out=rstd[m][:, lo:hi],
                in_=ss[m][:, lo:hi],
                func=ACT.Abs_reciprocal_sqrt,
                scale=1.0 / D,
                bias=eps_t[:, 0:1],
            )

        def ymul(m, i, on_vector=False):
            if i == 0:
                ys[m] = ypool.tile([P, 2, 2, 4, P], F32, name="y", align_bytes=64)
            src = x_tile(m, i).rearrange("p (c k t) -> p c t k", t=4, k=P)
            if on_vector:
                nc.vector.tensor_scalar(
                    out=ys[m][:, i], in0=src, scalar1=rstd[m][:, i : i + 1], scalar2=None, op0=ALU.mult
                )
            else:
                nc.gpsimd.tensor_scalar(
                    out=ys[m][:, i],
                    in0=src,
                    scalar1=rstd[m][:, i : i + 1],
                    scalar2=0.0,
                    op0=ALU.mult,
                    op1=ALU.add,
                )

        def trans(m, i):
            for c in range(2):
                yT = ps_t.tile([P, 4, P], F32, name="yT")
                yts[(m, i, c)] = yT
                for t in range(4):
                    nc.tensor.transpose(out=yT[:, t, :], in_=ys[m][:, i, c, t, :], identity=ident[:])

        def evac(m, i):
            if i == 0:
                grps[m] = gpool.tile([P, 2048], BF16, name="grp", align_bytes=64)
            for c in range(2):
                lo = (2 * i + c) * 512
                nc.vector.tensor_tensor(
                    out=grps[m][:, lo : lo + 512].rearrange("p (k i t) -> p k t i", i=2, t=4),
                    in0=yts[(m, i, c)][:].rearrange("p t (k i) -> p k t i", i=2),
                    in1=w4[:, c, :].unsqueeze(1).unsqueeze(3).to_broadcast([P, P // 2, 4, 2]),
                    op=ALU.mult,
                )

        def quant(m, i=0, tiles=2):
            if i == 0:
                cds[m] = (
                    gpool.tile([P, 512], U32, name="codes", align_bytes=64),
                    gpool.tile([P, 512], U8, name="scl", align_bytes=64),
                )
            codes, scl = cds[m]
            lo, hi = i * 256, (i + tiles) * 256
            nc.vector.quantize_mx(
                out=codes[:, lo:hi].bitcast(FP8X4), scales=scl[:, lo:hi], in_=grps[m][:, 4 * lo : 4 * hi]
            )

        def mx(m, i):
            po = ps_o.tile([P, 512], F32, name="po")
            pos[(m, i)] = po
            codes, scl = cds[m]
            nc.tensor.matmul(out=po[:, 0:WARM_COLS], lhsT=filler[:, 0:P], rhs=filler[:], start=True, stop=True)
            for c in range(2):
                lo = (2 * i + c) * P
                nc.tensor.matmul_mx(
                    out=po[:],
                    lhsT=codes[:, lo : lo + P].bitcast(FP8X4),
                    lhsT_scale=scl[:, lo : lo + P],
                    rhs=w_c[:, c * 512 : (c + 1) * 512].bitcast(FP8X4),
                    rhs_scale=w_s[:, c * 512 : (c + 1) * 512],
                    start=(c == 0),
                    stop=(c == 1),
                )

        def on_scalar(m):
            return V_TO <= m < LASTP

        def v_on_vector(m, i):
            return m < V_TO and i == 0 and m % 2 == 0

        def heads(m, i, lo=0, hi=4):
            g, jj = divmod(2 * m + i, GROUP)
            if i == 0 and lo == 0:
                ssqs[m] = small.tile([P, 8], F32, name="ssq")
            if jj == 0 and lo == 0:
                otile[g] = opool.tile([P, 6, GROUP, HD], F32, name="otile")
            for w in range(lo, hi):
                junk2 = junkp.tile([P, HD], BF16, name="junk2")
                nc.scalar.activation(
                    out=junk2[:],
                    in_=pos[(m, i)][:, w * HD : (w + 1) * HD],
                    func=ACT.Square,
                    accum_out=ssqs[m][:, i * 4 + w : i * 4 + w + 1],
                )
            if hi == 4 and not v_on_vector(m, i):
                nc.scalar.copy(
                    out=otile[g][:, 4:6, jj, :], in_=pos[(m, i)][:, 256:384].rearrange("p (w d) -> p w d", d=HD)
                )

        def root(m, i=0, tiles=2):
            nc.scalar.activation(
                out=rn[:, m % RN_SLOTS, i : i + tiles, 0:4],
                in_=ssqs[m][:, i * 4 : (i + tiles) * 4].rearrange("p (i w) -> p i w", w=4),
                func=ACT.Abs_reciprocal_sqrt,
                bias=tiny[:, 0:1],
            )

        def clip(m, i):
            r = rn[:, m % RN_SLOTS, i, 0:4]
            nc.gpsimd.tensor_scalar(out=r, in0=r, scalar1=1e12, scalar2=0.0, op0=ALU.min, op1=ALU.add)

        def scale_on_scalar(m, i):
            g, jj = divmod(2 * m + i, GROUP)
            for w in range(4):
                nc.scalar.activation(
                    out=otile[g][:, w, jj, :],
                    in_=pos[(m, i)][:, w * HD : (w + 1) * HD],
                    func=ACT.Copy,
                    scale=rn[:, m % RN_SLOTS, i, w : w + 1],
                )

        def scale(m, i):
            g, jj = divmod(2 * m + i, GROUP)
            h = 6 if v_on_vector(m, i) else 4
            nc.vector.scalar_tensor_tensor(
                out=otile[g][:, 0:h, jj, :],
                in0=rn[:, m % RN_SLOTS, i, 0:h].unsqueeze(2).to_broadcast([P, h, HD]),
                scalar=1e12,
                in1=pos[(m, i)][:, 0 : h * HD].rearrange("p (w d) -> p w d", d=HD),
                op0=ALU.min,
                op1=ALU.mult,
            )

        def store(g, lo, hi):
            b, j0 = divmod(g * GROUP, J)
            for m in (2, 0, 1):
                nc.sync.dma_start(
                    out=ov[m][b][:, :, j0 + lo : j0 + hi, :], in_=otile[g][:, 2 * m : 2 * m + 2, lo:hi, :]
                )

        def ok(m):
            return 0 <= m < N_PAIRS

        def keep_warm(count):
            wt = ps_o.tile([P, 512], F32, name="po")
            for k in range(count):
                nc.tensor.matmul(out=wt[:, 0:P], lhsT=ident[:], rhs=ident[:], start=True, stop=True)

        keep_warm(14)

        for n in range(-4, N_PAIRS + 1):
            if n >= 0 and n % 2 == 0 and n // 2 + X_BUFS < N_GROUPS:
                load(n // 2 + X_BUFS)
            if ok(n - 1):
                heads(n - 1, 1, 0, RMS_AT)
            if ok(n + 3) and n + 3 >= ONE_BY_ONE:
                rms(n + 3, 0, 2)
            if ok(n - 1):
                heads(n - 1, 1, RMS_AT, 4)
            if ok(n) and n != LASTP:
                quant(n)
            if ok(n + 3):
                if n + 3 == 0:
                    regroup_weights(0)
                ymul(n + 3, 0, on_vector=(n + 3 == 0))
                if n + 3 == 0:
                    regroup_weights(1)
                    quant_weights()
                ymul(n + 3, 1, on_vector=(n + 3 == 0))
            if ok(n) and n != LASTP:
                mx(n, 0)
            if ok(n + 4):
                sumsq(n + 4, 0)
                if n + 4 < ONE_BY_ONE:
                    rms(n + 4, 0, 1)
            if n == N_PAIRS:
                scale(LASTP, 0)
                root(LASTP, 1, 1)
            elif ok(n - 1):
                root(n - 1)
                if on_scalar(n - 1):
                    clip(n - 1, 1)
            if ok(n + 1):
                evac(n + 1, 0)
            if n + 1 == LASTP:
                scale(n - 1, 0)
                quant(n + 1, 0, 1)
            if ok(n + 2):
                trans(n + 2, 0)
            if n + 2 == 0:
                keep_warm(5)
            if n + 2 == 1:
                keep_warm(2)
            if ok(n):
                mx(n, 1)
            if n + 1 == LASTP:
                mx(n + 1, 0)
            if ok(n):
                heads(n, 0)
            if on_scalar(n - 1):
                scale_on_scalar(n - 1, 1)
            if n == LASTP:
                root(LASTP, 0, 1)
            if ok(n + 4):
                sumsq(n + 4, 1)
                if n + 4 < ONE_BY_ONE:
                    rms(n + 4, 1, 2)
            if ok(n + 1):
                evac(n + 1, 1)
            if n + 1 == LASTP:
                quant(n + 1, 1, 1)
            if ok(n + 2):
                trans(n + 2, 1)
            if n + 2 == 0:
                keep_warm(2)
            if n + 2 == 1:
                keep_warm(2)
            if ok(n - 1):
                if n + 1 != LASTP and n != N_PAIRS:
                    scale(n - 1, 0)
                if not on_scalar(n - 1):
                    scale(n - 1, 1)
                g_out, odd = divmod(n - 1, 2)
                if n == N_PAIRS:
                    store(g_out, 2, 3)
                    store(g_out, 3, 4)
                elif g_out == N_GROUPS - 1:
                    store(g_out, 2 * odd, 2 * odd + 2)
                elif odd:
                    store(g_out, 0, GROUP)
